import numpy as np
import ml_dtypes


def mxq(x, axis, fmt="e4m3"):
    dtype, down = {"e4m3": (ml_dtypes.float8_e4m3fn, 7), "e5m2": (ml_dtypes.float8_e5m2, 14)}[fmt]
    v = np.moveaxis(np.asarray(x, np.float32).astype(ml_dtypes.bfloat16).astype(np.float64), axis, -1)
    blocks = v.reshape(v.shape[:-1] + (-1, 32))
    amax = np.abs(blocks).max(-1, keepdims=True)
    byte = np.maximum(np.where(amax > 0, np.frexp(amax)[1] - 1 + 127, 0) - down, 1)
    scale = np.exp2(byte - 127.0)
    codes = (blocks / scale).astype(np.float32).astype(dtype).astype(np.float64)
    return np.moveaxis((codes * scale).reshape(v.shape), -1, axis)


WIDE = False


def mx_kscale(k):
    if not WIDE:
        return np.ones(k)
    levels = np.array([10, -10, 5, -5, 0])
    a = np.random.permutation(np.resize(levels, k // 512 * 4)).reshape(k // 512, 4)
    idx = np.arange(k)
    return np.exp2(a[idx // 512, idx % 128 // 32])


BF16 = ml_dtypes.bfloat16


def bf(x):
    return np.asarray(x, np.float32).astype(BF16)


def f64(x):
    return np.asarray(x).astype(np.float64)


E2M1 = np.array([0.0, 0.5, 1.0, 1.5, 2.0, 3.0, 4.0, 6.0, -0.0, -0.5, -1.0, -1.5, -2.0, -3.0, -4.0, -6.0])


def pack_weight(w, fmt):
    k, n = w.shape
    w = f64(bf(w)).reshape(k // 32, 32, n)
    amax = np.abs(w).max(1)
    if fmt == "e4m3":
        byte = np.frexp(amax)[1] - 1 + 127 - 7
    else:
        mant, ex = np.frexp(amax / 6.0)
        byte = np.where(mant > 0.5, ex, ex - 1) + 127
    byte = np.clip(np.where(amax > 0, byte, 1), 1, 254)
    scaled = (w * np.exp2(127.0 - byte)[:, None, :]).reshape(k, n).astype(np.float32)
    by_word = np.ascontiguousarray(scaled.reshape(k // 512, 128, 4, n).transpose(0, 1, 3, 2))
    if fmt == "e4m3":
        words = by_word.astype(ml_dtypes.float8_e4m3fn).view(np.uint8)
    else:
        c = by_word.astype(ml_dtypes.float4_e2m1fn).view(np.uint8) & 0xF
        words = c[..., 0::2] | (c[..., 1::2] << 4)
    return np.ascontiguousarray(words), np.ascontiguousarray(byte.astype(np.uint8).reshape(k // 512, 16, n))


def unpack_weight(words, scales, fmt):
    g, p, n, _ = words.shape
    if fmt == "e4m3":
        vals = np.ascontiguousarray(words).view(ml_dtypes.float8_e4m3fn).astype(np.float64)
    else:
        nib = np.empty((g, p, n, 4), np.uint8)
        nib[..., 0::2] = words & 0xF
        nib[..., 1::2] = words >> 4
        vals = E2M1[nib]
    vals = vals * np.repeat(np.exp2(scales.astype(np.float64) - 127.0), 8, axis=1)[..., None]
    return vals.transpose(0, 1, 3, 2).reshape(g * 512, n)


N, D, C, M = 3072, 512, 16, 16
LAMDA = 0.00390625
VS = 1.0 / (LAMDA * D)


def setup_inputs():
    s = mx_kscale(D)
    x = bf(np.random.standard_normal((N, D)) * s)
    x_var = bf(np.random.uniform(0.0, 1.0, (N, D)) * (0.5 + np.random.uniform(0.0, 1.0, (N, 1))) * 2.0 * VS)
    pm = np.random.standard_normal((C, M, D)) / np.sqrt(D) / s
    cat = np.ascontiguousarray(pm.swapaxes(1, 2)).reshape(-1, M)
    words, scales = pack_weight(cat, "e4m3")
    proto_var = bf(np.random.uniform(0.0, 1.0, (C, M, D)) * (0.5 + np.random.uniform(0.0, 1.0, (C, M, 1))) * 2.0 * VS)
    return {"x": x,
            "x_var": x_var,
            "proto_mean_words": words,
            "proto_mean_scales": scales,
            "proto_var": proto_var}


def reference(x, x_var, proto_mean_words, proto_mean_scales, proto_var):
    xv, pv = f64(x_var), f64(proto_var)
    dot = (mxq(f64(x), 1, "e4m3") @ unpack_weight(proto_mean_words, proto_mean_scales, "e4m3").reshape(C, D, M).swapaxes(1, 2).reshape(C * M, D).T).reshape(N, C, M)
    cross = (mxq(np.sqrt(xv), 1, "e4m3") @ mxq(np.sqrt(pv), 2, "e4m3").reshape(C * M, D).T).reshape(N, C, M)
    var_term = xv.sum(-1)[:, None, None] + pv.sum(-1)[None, :, :] - 2.0 * cross
    return -(2.0 - 2.0 * dot + LAMDA * var_term)

@@ -1,0 +1,214 @@
+from contextlib import ExitStack
+
+import concourse.mybir as mybir
+from concourse.masks import make_identity
+
+F32 = mybir.dt.float32
+BF16 = mybir.dt.bfloat16
+I32 = mybir.dt.int32
+U32 = mybir.dt.uint32
+U8 = mybir.dt.uint8
+FP8X4 = mybir.dt.float8_e4m3fn_x4
+ACT = mybir.ActivationFunctionType
+ALU = mybir.AluOpType
+
+P = 128
+N_ROWS = 3072
+D = 512
+N_CLASSES = 16
+N_PROTOS = 16
+J = N_CLASSES * N_PROTOS
+LAMDA = 0.00390625
+
+WORDS = D // 2
+HALVES = 2
+PAIR = 2
+PAIR_COLS = PAIR * P
+CHUNK = 4
+N_CHUNKS = N_ROWS // (CHUNK * P)
+N_PAIRS = N_ROWS // (PAIR * P)
+PAIRS_IN_CHUNK = CHUNK // PAIR
+
+FLOPS = 2 * 2 * N_ROWS * D * J
+
+
+def tile_probprotoseghead_e_kernel(
+    tc, x, x_var, proto_mean_words, proto_mean_scales, proto_var, out
+):
+    nc = tc.nc
+
+    x_chunks = x.rearrange("(k p t) d -> k p t d", p=P, t=CHUNK)
+    xv_chunks = x_var.rearrange("(k p t) d -> k p t d", p=P, t=CHUNK)
+    out_chunks = out.rearrange("n c m -> n (c m)").rearrange("(k p t) j -> k p t j", p=P, t=CHUNK)
+
+    with ExitStack() as ctx:
+        const = ctx.enter_context(tc.tile_pool(name="const", bufs=1))
+        rows = ctx.enter_context(tc.tile_pool(name="rows", bufs=N_CHUNKS))
+        work = ctx.enter_context(tc.tile_pool(name="work", bufs=3))
+        psum = ctx.enter_context(tc.psum_pool(name="psum", bufs=2))
+        psum_once = ctx.enter_context(tc.psum_pool(name="psum_once", bufs=1))
+
+        pm_scales = const.tile([P, J], U8, align_bytes=64)
+        nc.vector.memset(pm_scales[:].bitcast(I32), 0)
+        scale_words = proto_mean_scales.bitcast(I32)
+        for quadrant in range(4):
+            nc.sync.dma_start(
+                out=pm_scales[32 * quadrant : 32 * quadrant + 4, :]
+                .bitcast(I32)
+                .rearrange("r (c w) -> r c w", c=N_CLASSES),
+                in_=scale_words[:, 4 * quadrant : 4 * quadrant + 4, :].rearrange("c r w -> r c w"),
+            )
+        pm_codes = const.tile([P, J], U32, align_bytes=64)
+        nc.sync.dma_start(
+            out=pm_codes[:].bitcast(I32).rearrange("p (c m) -> p c m", c=N_CLASSES),
+            in_=proto_mean_words.rearrange("c p m t -> p c (m t)").bitcast(I32),
+        )
+        pv_rows = const.tile([P, PAIR, D], BF16)
+        nc.sync.dma_start(
+            out=pv_rows[:],
+            in_=proto_var.rearrange("c m d -> (c m) d").rearrange("(i p) d -> p i d", p=P),
+        )
+        x_rows = []
+        xv_rows = []
+        for k in range(N_CHUNKS):
+            xv_tile = rows.tile([P, CHUNK, D], BF16, name="xv_rows")
+            nc.sync.dma_start(out=xv_tile[:], in_=xv_chunks[k])
+            xv_rows.append(xv_tile)
+            x_tile = rows.tile([P, CHUNK, D], BF16, name="x_rows")
+            nc.sync.dma_start(out=x_tile[:], in_=x_chunks[k])
+            x_rows.append(x_tile)
+
+        identity = const.tile([P, P], F32)
+        make_identity(nc, identity[:])
+
+        def row_sums(sums, source, n_tiles):
+            for t in range(n_tiles):
+                folded = work.tile([P, D // 2], F32, name="folded")
+                nc.vector.scalar_tensor_tensor(
+                    out=folded[:],
+                    in0=source[:, t, 0 : D // 2],
+                    scalar=1.0,
+                    in1=source[:, t, D // 2 : D],
+                    op0=ALU.mult,
+                    op1=ALU.add,
+                    accum_out=sums[:, t : t + 1],
+                )
+
+        def transpose_words(bank, source, first_tile, interleaved):
+            words = source[:].bitcast(F32)
+            for i in range(PAIR):
+                for u in range(HALVES):
+                    if interleaved:
+                        picked = words[:, first_tile + i, u:WORDS:HALVES]
+                    else:
+                        picked = words[:, first_tile + i, u * P : (u + 1) * P]
+                    nc.tensor.transpose(bank[:, u, i * P : (i + 1) * P], picked, identity[:])
+
+        def quantise(grouped, name):
+            codes = work.tile([P, PAIR_COLS], U32, name=name + "_codes", align_bytes=64)
+            scales = work.tile([P, PAIR_COLS], U8, name=name + "_scales", align_bytes=64)
+            nc.vector.quantize_mx(
+                out=codes[:].bitcast(FP8X4),
+                scales=scales[:],
+                in_=grouped[:].rearrange("p r t -> p (r t)"),
+            )
+            return codes, scales
+
+        def sqrt_transposed(source, first_tile, scale, name):
+            bank = psum.tile([P, HALVES, PAIR_COLS], F32, name="var_bank")
+            transpose_words(bank, source, first_tile, interleaved=False)
+            grouped = work.tile([P, PAIR_COLS, 2 * HALVES], BF16, name="var_grouped", align_bytes=64)
+            nc.scalar.activation(
+                out=grouped[:].rearrange("p r (u e) -> p r u e", e=2),
+                in_=bank[:].bitcast(BF16).rearrange("p u (r e) -> p r u e", e=2),
+                func=ACT.Sqrt,
+                scale=scale,
+            )
+            return quantise(grouped, name)
+
+        pv_codes, pv_scales = sqrt_transposed(pv_rows, 0, LAMDA * LAMDA, "pv")
+
+        sp = const.tile([P, PAIR], F32)
+        row_sums(sp, pv_rows, PAIR)
+        sp_bias = const.tile([P, PAIR], F32)
+        nc.vector.tensor_scalar(
+            out=sp_bias[:], in0=sp[:], scalar1=-LAMDA, scalar2=-2.0, op0=ALU.mult, op1=ALU.add
+        )
+        bias_bank = psum_once.tile([P, J], F32)
+        for i in range(PAIR):
+            nc.tensor.transpose(
+                bias_bank[:, i * P : (i + 1) * P],
+                sp_bias[:, i : i + 1].to_broadcast([P, P]),
+                identity[:],
+            )
+        col_bias = const.tile([P, J], F32)
+        nc.vector.tensor_copy(out=col_bias[:], in_=bias_bank[:])
+
+        operands = {}
+        biases = {}
+        results = {}
+
+        def prepare(pair):
+            k, first_tile = pair // PAIRS_IN_CHUNK, PAIR * (pair % PAIRS_IN_CHUNK)
+            if first_tile == 0:
+                sx = work.tile([P, CHUNK], F32, name="sx")
+                row_sums(sx, xv_rows[k], CHUNK)
+                row_bias = work.tile([P, CHUNK], F32, name="row_bias")
+                nc.vector.tensor_scalar_mul(out=row_bias[:], in0=sx[:], scalar1=-LAMDA)
+                bias = work.tile([P, CHUNK, J], F32, name="bias")
+                for t in range(CHUNK):
+                    nc.vector.tensor_scalar_add(
+                        out=bias[:, t, :], in0=col_bias[:], scalar1=row_bias[:, t : t + 1]
+                    )
+                biases[k] = bias
+                results[k] = work.tile([P, CHUNK, J], F32, name="result")
+            xv_codes, xv_scales = sqrt_transposed(xv_rows[k], first_tile, 1.0, "xv")
+            x_bank = psum.tile([P, HALVES, PAIR_COLS], F32, name="x_bank")
+            transpose_words(x_bank, x_rows[k], first_tile, interleaved=True)
+            x_grouped = work.tile([P, PAIR_COLS, 2 * HALVES], BF16, name="x_grouped", align_bytes=64)
+            nc.scalar.copy(
+                out=x_grouped[:].bitcast(F32), in_=x_bank[:].rearrange("p u r -> p r u")
+            )
+            x_codes, x_scales = quantise(x_grouped, "x")
+            operands[pair] = (x_codes, x_scales, xv_codes, xv_scales)
+
+        def multiply(pair):
+            k, first_tile = pair // PAIRS_IN_CHUNK, PAIR * (pair % PAIRS_IN_CHUNK)
+            x_codes, x_scales, xv_codes, xv_scales = operands[pair]
+            acc = psum.tile([P, PAIR, J], F32, name="acc")
+            for i in range(PAIR):
+                cols = slice(i * P, (i + 1) * P)
+                nc.tensor.matmul_mx(
+                    out=acc[:, i, :],
+                    lhsT=x_codes[:, cols].bitcast(FP8X4),
+                    lhsT_scale=x_scales[:, cols],
+                    rhs=pm_codes[:].bitcast(FP8X4),
+                    rhs_scale=pm_scales[:],
+                    start=True,
+                    stop=False,
+                )
+                nc.tensor.matmul_mx(
+                    out=acc[:, i, :],
+                    lhsT=xv_codes[:, cols].bitcast(FP8X4),
+                    lhsT_scale=xv_scales[:, cols],
+                    rhs=pv_codes[:].bitcast(FP8X4),
+                    rhs_scale=pv_scales[:],
+                    start=False,
+                    stop=True,
+                )
+            tiles = slice(first_tile, first_tile + PAIR)
+            nc.vector.scalar_tensor_tensor(
+                out=results[k][:, tiles, :].rearrange("p t j -> p (t j)"),
+                in0=acc[:].rearrange("p t j -> p (t j)"),
+                scalar=2.0,
+                in1=biases[k][:, tiles, :].rearrange("p t j -> p (t j)"),
+                op0=ALU.mult,
+                op1=ALU.add,
+            )
+            nc.sync.dma_start(out=out_chunks[k][:, tiles, :], in_=results[k][:, tiles, :])
+
+        prepare(0)
+        for pair in range(1, N_PAIRS):
+            prepare(pair)
+            multiply(pair - 1)
+        multiply(N_PAIRS - 1)

@@ -24,10 +24,7 @@ WORDS = D // 2
 HALVES = 2
 PAIR = 2
 PAIR_COLS = PAIR * P
-CHUNK = 4
-N_CHUNKS = N_ROWS // (CHUNK * P)
-N_PAIRS = N_ROWS // (PAIR * P)
-PAIRS_IN_CHUNK = CHUNK // PAIR
+N_PAIRS = N_ROWS // PAIR_COLS
 
 FLOPS = 2 * 2 * N_ROWS * D * J
 
@@ -37,17 +34,35 @@ def tile_probprotoseghead_e_kernel(
 ):
     nc = tc.nc
 
-    x_chunks = x.rearrange("(k p t) d -> k p t d", p=P, t=CHUNK)
-    xv_chunks = x_var.rearrange("(k p t) d -> k p t d", p=P, t=CHUNK)
-    out_chunks = out.rearrange("n c m -> n (c m)").rearrange("(k p t) j -> k p t j", p=P, t=CHUNK)
+    x_pairs = x.rearrange("(s p t) d -> s p t d", p=P, t=PAIR)
+    xv_pairs = x_var.rearrange("(s p t) d -> s p t d", p=P, t=PAIR)
+    out_pairs = out.rearrange("n c m -> n (c m)").rearrange("(s p t) j -> s p t j", p=P, t=PAIR)
 
     with ExitStack() as ctx:
         const = ctx.enter_context(tc.tile_pool(name="const", bufs=1))
-        rows = ctx.enter_context(tc.tile_pool(name="rows", bufs=N_CHUNKS))
-        work = ctx.enter_context(tc.tile_pool(name="work", bufs=3))
+        rows = ctx.enter_context(tc.tile_pool(name="rows", bufs=N_PAIRS))
+        work = ctx.enter_context(tc.tile_pool(name="work", bufs=4))
         psum = ctx.enter_context(tc.psum_pool(name="psum", bufs=2))
         psum_once = ctx.enter_context(tc.psum_pool(name="psum_once", bufs=1))
+        ctx.enter_context(tc.manual_schedule())
 
+        pv_rows = const.tile([P, PAIR, D], BF16)
+        nc.sync.dma_start(
+            out=pv_rows[:],
+            in_=proto_var.rearrange("c m d -> (c m) d").rearrange("(i p) d -> p i d", p=P),
+        )
+        x_rows = []
+        xv_rows = []
+
+        def load_pair(s):
+            xv_tile = rows.tile([P, PAIR, D], BF16, name="xv_rows")
+            nc.sync.dma_start(out=xv_tile[:], in_=xv_pairs[s])
+            xv_rows.append(xv_tile)
+            x_tile = rows.tile([P, PAIR, D], BF16, name="x_rows")
+            nc.sync.dma_start(out=x_tile[:], in_=x_pairs[s])
+            x_rows.append(x_tile)
+
+        load_pair(0)
         pm_scales = const.tile([P, J], U8, align_bytes=64)
         nc.vector.memset(pm_scales[:].bitcast(I32), 0)
         scale_words = proto_mean_scales.bitcast(I32)
@@ -63,26 +78,14 @@ def tile_probprotoseghead_e_kernel(
             out=pm_codes[:].bitcast(I32).rearrange("p (c m) -> p c m", c=N_CLASSES),
             in_=proto_mean_words.rearrange("c p m t -> p c (m t)").bitcast(I32),
         )
-        pv_rows = const.tile([P, PAIR, D], BF16)
-        nc.sync.dma_start(
-            out=pv_rows[:],
-            in_=proto_var.rearrange("c m d -> (c m) d").rearrange("(i p) d -> p i d", p=P),
-        )
-        x_rows = []
-        xv_rows = []
-        for k in range(N_CHUNKS):
-            xv_tile = rows.tile([P, CHUNK, D], BF16, name="xv_rows")
-            nc.sync.dma_start(out=xv_tile[:], in_=xv_chunks[k])
-            xv_rows.append(xv_tile)
-            x_tile = rows.tile([P, CHUNK, D], BF16, name="x_rows")
-            nc.sync.dma_start(out=x_tile[:], in_=x_chunks[k])
-            x_rows.append(x_tile)
+        for s in range(1, N_PAIRS):
+            load_pair(s)
 
         identity = const.tile([P, P], F32)
         make_identity(nc, identity[:])
 
-        def row_sums(sums, source, n_tiles):
-            for t in range(n_tiles):
+        def row_sums(sums, source):
+            for t in range(PAIR):
                 folded = work.tile([P, D // 2], F32, name="folded")
                 nc.vector.scalar_tensor_tensor(
                     out=folded[:],
@@ -94,19 +97,20 @@ def tile_probprotoseghead_e_kernel(
                     accum_out=sums[:, t : t + 1],
                 )
 
-        def transpose_words(bank, source, first_tile, interleaved):
+        def transpose_words(bank, source, interleaved):
             words = source[:].bitcast(F32)
             for i in range(PAIR):
                 for u in range(HALVES):
                     if interleaved:
-                        picked = words[:, first_tile + i, u:WORDS:HALVES]
+                        picked = words[:, i, u:WORDS:HALVES]
                     else:
-                        picked = words[:, first_tile + i, u * P : (u + 1) * P]
+                        picked = words[:, i, u * P : (u + 1) * P]
                     nc.tensor.transpose(bank[:, u, i * P : (i + 1) * P], picked, identity[:])
 
-        def quantise(grouped, name):
-            codes = work.tile([P, PAIR_COLS], U32, name=name + "_codes", align_bytes=64)
-            scales = work.tile([P, PAIR_COLS], U8, name=name + "_scales", align_bytes=64)
+        def quantise(pool, grouped, name):
+            columns = grouped.shape[1]
+            codes = pool.tile([P, columns], U32, name=name + "_codes", align_bytes=64)
+            scales = pool.tile([P, columns], U8, name=name + "_scales", align_bytes=64)
             nc.vector.quantize_mx(
                 out=codes[:].bitcast(FP8X4),
                 scales=scales[:],
@@ -114,74 +118,77 @@ def tile_probprotoseghead_e_kernel(
             )
             return codes, scales
 
-        def sqrt_transposed(source, first_tile, scale, name):
+        def sqrt_transposed(grouped, source, scale):
             bank = psum.tile([P, HALVES, PAIR_COLS], F32, name="var_bank")
-            transpose_words(bank, source, first_tile, interleaved=False)
-            grouped = work.tile([P, PAIR_COLS, 2 * HALVES], BF16, name="var_grouped", align_bytes=64)
+            transpose_words(bank, source, interleaved=False)
             nc.scalar.activation(
-                out=grouped[:].rearrange("p r (u e) -> p r u e", e=2),
+                out=grouped.rearrange("p r (u e) -> p r u e", e=2),
                 in_=bank[:].bitcast(BF16).rearrange("p u (r e) -> p r u e", e=2),
                 func=ACT.Sqrt,
                 scale=scale,
             )
-            return quantise(grouped, name)
 
-        pv_codes, pv_scales = sqrt_transposed(pv_rows, 0, LAMDA * LAMDA, "pv")
+        pv_grouped = const.tile([P, PAIR_COLS, 2 * HALVES], BF16, align_bytes=64)
+        sqrt_transposed(pv_grouped[:], pv_rows, LAMDA * LAMDA)
 
         sp = const.tile([P, PAIR], F32)
-        row_sums(sp, pv_rows, PAIR)
-        sp_bias = const.tile([P, PAIR], F32)
-        nc.vector.tensor_scalar(
-            out=sp_bias[:], in0=sp[:], scalar1=-LAMDA, scalar2=-2.0, op0=ALU.mult, op1=ALU.add
-        )
-        bias_bank = psum_once.tile([P, J], F32)
+        row_sums(sp, pv_rows)
+        sp_shifted = const.tile([P, PAIR], F32)
+        nc.vector.tensor_scalar_add(out=sp_shifted[:], in0=sp[:], scalar1=2.0 / LAMDA)
+        col_bank = psum_once.tile([P, J], F32)
         for i in range(PAIR):
             nc.tensor.transpose(
-                bias_bank[:, i * P : (i + 1) * P],
-                sp_bias[:, i : i + 1].to_broadcast([P, P]),
+                col_bank[:, i * P : (i + 1) * P],
+                sp_shifted[:, i : i + 1].to_broadcast([P, P]),
                 identity[:],
             )
-        col_bias = const.tile([P, J], F32)
-        nc.vector.tensor_copy(out=col_bias[:], in_=bias_bank[:])
+        col_sum = const.tile([P, J], F32)
+        nc.vector.tensor_copy(out=col_sum[:], in_=col_bank[:])
+        pv_codes, pv_scales = quantise(const, pv_grouped, "pv")
 
-        operands = {}
-        biases = {}
-        results = {}
+        grouped_of = {}
+        codes_of = {}
+        bias_of = {}
 
-        def prepare(pair):
-            k, first_tile = pair // PAIRS_IN_CHUNK, PAIR * (pair % PAIRS_IN_CHUNK)
-            if first_tile == 0:
-                sx = work.tile([P, CHUNK], F32, name="sx")
-                row_sums(sx, xv_rows[k], CHUNK)
-                row_bias = work.tile([P, CHUNK], F32, name="row_bias")
-                nc.vector.tensor_scalar_mul(out=row_bias[:], in0=sx[:], scalar1=-LAMDA)
-                bias = work.tile([P, CHUNK, J], F32, name="bias")
-                for t in range(CHUNK):
-                    nc.vector.tensor_scalar_add(
-                        out=bias[:, t, :], in0=col_bias[:], scalar1=row_bias[:, t : t + 1]
-                    )
-                biases[k] = bias
-                results[k] = work.tile([P, CHUNK, J], F32, name="result")
-            xv_codes, xv_scales = sqrt_transposed(xv_rows[k], first_tile, 1.0, "xv")
+        def transpose_pair(s):
+            grouped = work.tile([P, 2 * PAIR_COLS, 2 * HALVES], BF16, name="grouped", align_bytes=64)
+            sqrt_transposed(grouped[:, 0:PAIR_COLS, :], xv_rows[s], 1.0)
             x_bank = psum.tile([P, HALVES, PAIR_COLS], F32, name="x_bank")
-            transpose_words(x_bank, x_rows[k], first_tile, interleaved=True)
-            x_grouped = work.tile([P, PAIR_COLS, 2 * HALVES], BF16, name="x_grouped", align_bytes=64)
+            transpose_words(x_bank, x_rows[s], interleaved=True)
             nc.scalar.copy(
-                out=x_grouped[:].bitcast(F32), in_=x_bank[:].rearrange("p u r -> p r u")
+                out=grouped[:, PAIR_COLS : 2 * PAIR_COLS, :].bitcast(F32),
+                in_=x_bank[:].rearrange("p u r -> p r u"),
             )
-            x_codes, x_scales = quantise(x_grouped, "x")
-            operands[pair] = (x_codes, x_scales, xv_codes, xv_scales)
+            grouped_of[s] = grouped
 
-        def multiply(pair):
-            k, first_tile = pair // PAIRS_IN_CHUNK, PAIR * (pair % PAIRS_IN_CHUNK)
-            x_codes, x_scales, xv_codes, xv_scales = operands[pair]
+        def bias_pair(s):
+            sx = work.tile([P, PAIR], F32, name="sx")
+            row_sums(sx, xv_rows[s])
+            bias = work.tile([P, PAIR, J], F32, name="bias")
+            for t in range(PAIR):
+                nc.gpsimd.tensor_scalar(
+                    out=bias[:, t, :],
+                    in0=col_sum[:],
+                    scalar1=sx[:, t : t + 1],
+                    scalar2=-LAMDA,
+                    op0=ALU.add,
+                    op1=ALU.mult,
+                )
+            bias_of[s] = bias
+
+        def quantise_pair(s):
+            codes_of[s] = quantise(work, grouped_of[s], "pixel")
+
+        def multiply_pair(s):
+            codes, scales = codes_of[s]
             acc = psum.tile([P, PAIR, J], F32, name="acc")
             for i in range(PAIR):
-                cols = slice(i * P, (i + 1) * P)
+                xv_cols = slice(i * P, (i + 1) * P)
+                x_cols = slice(PAIR_COLS + i * P, PAIR_COLS + (i + 1) * P)
                 nc.tensor.matmul_mx(
                     out=acc[:, i, :],
-                    lhsT=x_codes[:, cols].bitcast(FP8X4),
-                    lhsT_scale=x_scales[:, cols],
+                    lhsT=codes[:, x_cols].bitcast(FP8X4),
+                    lhsT_scale=scales[:, x_cols],
                     rhs=pm_codes[:].bitcast(FP8X4),
                     rhs_scale=pm_scales[:],
                     start=True,
@@ -189,26 +196,29 @@ def tile_probprotoseghead_e_kernel(
                 )
                 nc.tensor.matmul_mx(
                     out=acc[:, i, :],
-                    lhsT=xv_codes[:, cols].bitcast(FP8X4),
-                    lhsT_scale=xv_scales[:, cols],
+                    lhsT=codes[:, xv_cols].bitcast(FP8X4),
+                    lhsT_scale=scales[:, xv_cols],
                     rhs=pv_codes[:].bitcast(FP8X4),
                     rhs_scale=pv_scales[:],
                     start=False,
                     stop=True,
                 )
-            tiles = slice(first_tile, first_tile + PAIR)
+            result = work.tile([P, PAIR, J], F32, name="result")
             nc.vector.scalar_tensor_tensor(
-                out=results[k][:, tiles, :].rearrange("p t j -> p (t j)"),
+                out=result[:].rearrange("p t j -> p (t j)"),
                 in0=acc[:].rearrange("p t j -> p (t j)"),
                 scalar=2.0,
-                in1=biases[k][:, tiles, :].rearrange("p t j -> p (t j)"),
+                in1=bias_of[s][:].rearrange("p t j -> p (t j)"),
                 op0=ALU.mult,
                 op1=ALU.add,
             )
-            nc.sync.dma_start(out=out_chunks[k][:, tiles, :], in_=results[k][:, tiles, :])
+            nc.sync.dma_start(out=out_pairs[s], in_=result[:])
 
-        prepare(0)
-        for pair in range(1, N_PAIRS):
-            prepare(pair)
-            multiply(pair - 1)
-        multiply(N_PAIRS - 1)
+        for step in range(N_PAIRS + 2):
+            if step < N_PAIRS:
+                transpose_pair(step)
+                bias_pair(step)
+            if 1 <= step <= N_PAIRS:
+                quantise_pair(step - 1)
+            if step >= 2:
+                multiply_pair(step - 2)

@@ -129,21 +129,23 @@ def tile_probprotoseghead_e_kernel(
             )
 
         pv_grouped = const.tile([P, PAIR_COLS, 2 * HALVES], BF16, align_bytes=64)
-        sqrt_transposed(pv_grouped[:], pv_rows, LAMDA * LAMDA)
+        sqrt_transposed(pv_grouped[:], pv_rows, 4.0 * LAMDA * LAMDA)
 
         sp = const.tile([P, PAIR], F32)
         row_sums(sp, pv_rows)
-        sp_shifted = const.tile([P, PAIR], F32)
-        nc.vector.tensor_scalar_add(out=sp_shifted[:], in0=sp[:], scalar1=2.0 / LAMDA)
+        sp_bias = const.tile([P, PAIR], F32)
+        nc.vector.tensor_scalar(
+            out=sp_bias[:], in0=sp[:], scalar1=-LAMDA, scalar2=-2.0, op0=ALU.mult, op1=ALU.add
+        )
         col_bank = psum_once.tile([P, J], F32)
         for i in range(PAIR):
             nc.tensor.transpose(
                 col_bank[:, i * P : (i + 1) * P],
-                sp_shifted[:, i : i + 1].to_broadcast([P, P]),
+                sp_bias[:, i : i + 1].to_broadcast([P, P]),
                 identity[:],
             )
-        col_sum = const.tile([P, J], F32)
-        nc.vector.tensor_copy(out=col_sum[:], in_=col_bank[:])
+        col_bias = const.tile([P, J], F32)
+        nc.vector.tensor_copy(out=col_bias[:], in_=col_bank[:])
         pv_codes, pv_scales = quantise(const, pv_grouped, "pv")
 
         grouped_of = {}
@@ -164,17 +166,9 @@ def tile_probprotoseghead_e_kernel(
         def bias_pair(s):
             sx = work.tile([P, PAIR], F32, name="sx")
             row_sums(sx, xv_rows[s])
-            bias = work.tile([P, PAIR, J], F32, name="bias")
-            for t in range(PAIR):
-                nc.gpsimd.tensor_scalar(
-                    out=bias[:, t, :],
-                    in0=col_sum[:],
-                    scalar1=sx[:, t : t + 1],
-                    scalar2=-LAMDA,
-                    op0=ALU.add,
-                    op1=ALU.mult,
-                )
-            bias_of[s] = bias
+            row_bias = work.tile([P, PAIR], F32, name="row_bias")
+            nc.gpsimd.tensor_scalar_mul(out=row_bias[:], in0=sx[:], scalar1=-LAMDA)
+            bias_of[s] = row_bias
 
         def quantise_pair(s):
             codes_of[s] = quantise(work, grouped_of[s], "pixel")
@@ -185,15 +179,16 @@ def tile_probprotoseghead_e_kernel(
             for i in range(PAIR):
                 xv_cols = slice(i * P, (i + 1) * P)
                 x_cols = slice(PAIR_COLS + i * P, PAIR_COLS + (i + 1) * P)
-                nc.tensor.matmul_mx(
-                    out=acc[:, i, :],
-                    lhsT=codes[:, x_cols].bitcast(FP8X4),
-                    lhsT_scale=scales[:, x_cols],
-                    rhs=pm_codes[:].bitcast(FP8X4),
-                    rhs_scale=pm_scales[:],
-                    start=True,
-                    stop=False,
-                )
+                for first in (True, False):
+                    nc.tensor.matmul_mx(
+                        out=acc[:, i, :],
+                        lhsT=codes[:, x_cols].bitcast(FP8X4),
+                        lhsT_scale=scales[:, x_cols],
+                        rhs=pm_codes[:].bitcast(FP8X4),
+                        rhs_scale=pm_scales[:],
+                        start=first,
+                        stop=False,
+                    )
                 nc.tensor.matmul_mx(
                     out=acc[:, i, :],
                     lhsT=codes[:, xv_cols].bitcast(FP8X4),
@@ -204,14 +199,15 @@ def tile_probprotoseghead_e_kernel(
                     stop=True,
                 )
             result = work.tile([P, PAIR, J], F32, name="result")
-            nc.vector.scalar_tensor_tensor(
-                out=result[:].rearrange("p t j -> p (t j)"),
-                in0=acc[:].rearrange("p t j -> p (t j)"),
-                scalar=2.0,
-                in1=bias_of[s][:].rearrange("p t j -> p (t j)"),
-                op0=ALU.mult,
-                op1=ALU.add,
-            )
+            for t in range(PAIR):
+                nc.vector.scalar_tensor_tensor(
+                    out=result[:, t, :],
+                    in0=acc[:, t, :],
+                    scalar=bias_of[s][:, t : t + 1],
+                    in1=col_bias[:],
+                    op0=ALU.add,
+                    op1=ALU.add,
+                )
             nc.sync.dma_start(out=out_pairs[s], in_=result[:])
 
         for step in range(N_PAIRS + 2):

@@ -42,7 +42,9 @@ def tile_probprotoseghead_e_kernel(
         const = ctx.enter_context(tc.tile_pool(name="const", bufs=1))
         rows = ctx.enter_context(tc.tile_pool(name="rows", bufs=N_PAIRS))
         work = ctx.enter_context(tc.tile_pool(name="work", bufs=4))
+        small = ctx.enter_context(tc.tile_pool(name="small", bufs=8))
         psum = ctx.enter_context(tc.psum_pool(name="psum", bufs=2))
+        psum_acc = ctx.enter_context(tc.psum_pool(name="psum_acc", bufs=3))
         psum_once = ctx.enter_context(tc.psum_pool(name="psum_once", bufs=1))
         ctx.enter_context(tc.manual_schedule())
 
@@ -54,15 +56,19 @@ def tile_probprotoseghead_e_kernel(
         x_rows = []
         xv_rows = []
 
-        def load_pair(s):
+        def load_x_var(s):
             xv_tile = rows.tile([P, PAIR, D], BF16, name="xv_rows")
             nc.sync.dma_start(out=xv_tile[:], in_=xv_pairs[s])
             xv_rows.append(xv_tile)
+
+        def load_x(s):
             x_tile = rows.tile([P, PAIR, D], BF16, name="x_rows")
             nc.sync.dma_start(out=x_tile[:], in_=x_pairs[s])
             x_rows.append(x_tile)
 
-        load_pair(0)
+        load_x_var(0)
+        load_x_var(1)
+        load_x(0)
         pm_scales = const.tile([P, J], U8, align_bytes=64)
         nc.vector.memset(pm_scales[:].bitcast(I32), 0)
         scale_words = proto_mean_scales.bitcast(I32)
@@ -79,7 +85,9 @@ def tile_probprotoseghead_e_kernel(
             in_=proto_mean_words.rearrange("c p m t -> p c (m t)").bitcast(I32),
         )
         for s in range(1, N_PAIRS):
-            load_pair(s)
+            if s + 1 < N_PAIRS:
+                load_x_var(s + 1)
+            load_x(s)
 
         identity = const.tile([P, P], F32)
         make_identity(nc, identity[:])
@@ -164,9 +172,9 @@ def tile_probprotoseghead_e_kernel(
             grouped_of[s] = grouped
 
         def bias_pair(s):
-            sx = work.tile([P, PAIR], F32, name="sx")
+            sx = small.tile([P, PAIR], F32, name="sx")
             row_sums(sx, xv_rows[s])
-            row_bias = work.tile([P, PAIR], F32, name="row_bias")
+            row_bias = small.tile([P, PAIR], F32, name="row_bias")
             nc.gpsimd.tensor_scalar_mul(out=row_bias[:], in0=sx[:], scalar1=-LAMDA)
             bias_of[s] = row_bias
 
@@ -175,7 +183,7 @@ def tile_probprotoseghead_e_kernel(
 
         def multiply_pair(s):
             codes, scales = codes_of[s]
-            acc = psum.tile([P, PAIR, J], F32, name="acc")
+            acc = psum_acc.tile([P, PAIR, J], F32, name="acc")
             for i in range(PAIR):
                 xv_cols = slice(i * P, (i + 1) * P)
                 x_cols = slice(PAIR_COLS + i * P, PAIR_COLS + (i + 1) * P)
@@ -210,11 +218,13 @@ def tile_probprotoseghead_e_kernel(
                 )
             nc.sync.dma_start(out=out_pairs[s], in_=result[:])
 
-        for step in range(N_PAIRS + 2):
+        bias_pair(0)
+        for step in range(N_PAIRS + 3):
             if step < N_PAIRS:
                 transpose_pair(step)
-                bias_pair(step)
+            if step + 1 < N_PAIRS:
+                bias_pair(step + 1)
             if 1 <= step <= N_PAIRS:
                 quantise_pair(step - 1)
-            if step >= 2:
-                multiply_pair(step - 2)
+            if step >= 3:
+                multiply_pair(step - 3)

@@ -138,23 +138,8 @@ def tile_probprotoseghead_e_kernel(
 
         pv_grouped = const.tile([P, PAIR_COLS, 2 * HALVES], BF16, align_bytes=64)
         sqrt_transposed(pv_grouped[:], pv_rows, 4.0 * LAMDA * LAMDA)
-
         sp = const.tile([P, PAIR], F32)
         row_sums(sp, pv_rows)
-        sp_bias = const.tile([P, PAIR], F32)
-        nc.vector.tensor_scalar(
-            out=sp_bias[:], in0=sp[:], scalar1=-LAMDA, scalar2=-2.0, op0=ALU.mult, op1=ALU.add
-        )
-        col_bank = psum_once.tile([P, J], F32)
-        for i in range(PAIR):
-            nc.tensor.transpose(
-                col_bank[:, i * P : (i + 1) * P],
-                sp_bias[:, i : i + 1].to_broadcast([P, P]),
-                identity[:],
-            )
-        col_bias = const.tile([P, J], F32)
-        nc.vector.tensor_copy(out=col_bias[:], in_=col_bank[:])
-        pv_codes, pv_scales = quantise(const, pv_grouped, "pv")
 
         grouped_of = {}
         codes_of = {}
@@ -219,12 +204,30 @@ def tile_probprotoseghead_e_kernel(
             nc.sync.dma_start(out=out_pairs[s], in_=result[:])
 
         bias_pair(0)
-        for step in range(N_PAIRS + 3):
-            if step < N_PAIRS:
-                transpose_pair(step)
-            if step + 1 < N_PAIRS:
-                bias_pair(step + 1)
-            if 1 <= step <= N_PAIRS:
-                quantise_pair(step - 1)
-            if step >= 3:
-                multiply_pair(step - 3)
+        transpose_pair(0)
+
+        sp_bias = const.tile([P, PAIR], F32)
+        nc.vector.tensor_scalar(
+            out=sp_bias[:], in0=sp[:], scalar1=-LAMDA, scalar2=-2.0, op0=ALU.mult, op1=ALU.add
+        )
+        col_bank = psum_once.tile([P, J], F32)
+        for i in range(PAIR):
+            nc.tensor.transpose(
+                col_bank[:, i * P : (i + 1) * P],
+                sp_bias[:, i : i + 1].to_broadcast([P, P]),
+                identity[:],
+            )
+        bias_pair(1)
+        pv_codes, pv_scales = quantise(const, pv_grouped, "pv")
+        col_bias = const.tile([P, J], F32)
+        nc.vector.tensor_copy(out=col_bias[:], in_=col_bank[:])
+
+        for s in range(N_PAIRS + 2):
+            if s + 1 < N_PAIRS:
+                transpose_pair(s + 1)
+            if s + 2 < N_PAIRS:
+                bias_pair(s + 2)
+            if s < N_PAIRS:
+                quantise_pair(s)
+            if s >= 2:
+                multiply_pair(s - 2)

@@ -48,6 +48,9 @@ def tile_probprotoseghead_e_kernel(
         psum_once = ctx.enter_context(tc.psum_pool(name="psum_once", bufs=1))
         ctx.enter_context(tc.manual_schedule())
 
+        identity = const.tile([P, P], F32)
+        make_identity(nc, identity[:])
+
         pv_rows = const.tile([P, PAIR, D], BF16)
         nc.sync.dma_start(
             out=pv_rows[:],
@@ -71,26 +74,23 @@ def tile_probprotoseghead_e_kernel(
         load_x(0)
         pm_scales = const.tile([P, J], U8, align_bytes=64)
         nc.vector.memset(pm_scales[:].bitcast(I32), 0)
-        scale_words = proto_mean_scales.bitcast(I32)
+        scale_words = proto_mean_scales.bitcast(F32)
         for quadrant in range(4):
-            nc.sync.dma_start(
+            nc.scalar.dma_start(
                 out=pm_scales[32 * quadrant : 32 * quadrant + 4, :]
-                .bitcast(I32)
+                .bitcast(F32)
                 .rearrange("r (c w) -> r c w", c=N_CLASSES),
                 in_=scale_words[:, 4 * quadrant : 4 * quadrant + 4, :].rearrange("c r w -> r c w"),
             )
         pm_codes = const.tile([P, J], U32, align_bytes=64)
-        nc.sync.dma_start(
-            out=pm_codes[:].bitcast(I32).rearrange("p (c m) -> p c m", c=N_CLASSES),
-            in_=proto_mean_words.rearrange("c p m t -> p c (m t)").bitcast(I32),
+        nc.scalar.dma_start(
+            out=pm_codes[:].bitcast(F32).rearrange("p (c m) -> p c m", c=N_CLASSES),
+            in_=proto_mean_words.rearrange("c p m t -> p c (m t)").bitcast(F32),
         )
         for s in range(1, N_PAIRS):
             if s + 1 < N_PAIRS:
                 load_x_var(s + 1)
             load_x(s)
-
-        identity = const.tile([P, P], F32)
-        make_identity(nc, identity[:])
 
         def row_sums(sums, source):
             for t in range(PAIR):

from contextlib import ExitStack

import concourse.mybir as mybir
from concourse.masks import make_identity

F32 = mybir.dt.float32
BF16 = mybir.dt.bfloat16
I32 = mybir.dt.int32
U32 = mybir.dt.uint32
U8 = mybir.dt.uint8
FP8X4 = mybir.dt.float8_e4m3fn_x4
ACT = mybir.ActivationFunctionType
ALU = mybir.AluOpType

P = 128
N_ROWS = 3072
D = 512
N_CLASSES = 16
N_PROTOS = 16
J = N_CLASSES * N_PROTOS
LAMDA = 0.00390625

WORDS = D // 2
HALVES = 2
PAIR = 2
PAIR_COLS = PAIR * P
N_PAIRS = N_ROWS // PAIR_COLS

FLOPS = 2 * 2 * N_ROWS * D * J


def tile_probprotoseghead_e_kernel(
    tc, x, x_var, proto_mean_words, proto_mean_scales, proto_var, out
):
    nc = tc.nc

    x_pairs = x.rearrange("(s p t) d -> s p t d", p=P, t=PAIR)
    xv_pairs = x_var.rearrange("(s p t) d -> s p t d", p=P, t=PAIR)
    out_pairs = out.rearrange("n c m -> n (c m)").rearrange("(s p t) j -> s p t j", p=P, t=PAIR)

    with ExitStack() as ctx:
        const = ctx.enter_context(tc.tile_pool(name="const", bufs=1))
        rows = ctx.enter_context(tc.tile_pool(name="rows", bufs=N_PAIRS))
        work = ctx.enter_context(tc.tile_pool(name="work", bufs=4))
        small = ctx.enter_context(tc.tile_pool(name="small", bufs=8))
        psum = ctx.enter_context(tc.psum_pool(name="psum", bufs=2))
        psum_acc = ctx.enter_context(tc.psum_pool(name="psum_acc", bufs=3))
        psum_once = ctx.enter_context(tc.psum_pool(name="psum_once", bufs=1))
        ctx.enter_context(tc.manual_schedule())

        identity = const.tile([P, P], F32)
        make_identity(nc, identity[:])

        pv_rows = const.tile([P, PAIR, D], BF16)
        nc.sync.dma_start(
            out=pv_rows[:],
            in_=proto_var.rearrange("c m d -> (c m) d").rearrange("(i p) d -> p i d", p=P),
        )
        x_rows = []
        xv_rows = []

        def load_x_var(s):
            xv_tile = rows.tile([P, PAIR, D], BF16, name="xv_rows")
            nc.sync.dma_start(out=xv_tile[:], in_=xv_pairs[s])
            xv_rows.append(xv_tile)

        def load_x(s):
            x_tile = rows.tile([P, PAIR, D], BF16, name="x_rows")
            nc.sync.dma_start(out=x_tile[:], in_=x_pairs[s])
            x_rows.append(x_tile)

        load_x_var(0)
        load_x_var(1)
        load_x(0)
        pm_scales = const.tile([P, J], U8, align_bytes=64)
        nc.vector.memset(pm_scales[:].bitcast(I32), 0)
        scale_words = proto_mean_scales.bitcast(F32)
        for quadrant in range(4):
            nc.scalar.dma_start(
                out=pm_scales[32 * quadrant : 32 * quadrant + 4, :]
                .bitcast(F32)
                .rearrange("r (c w) -> r c w", c=N_CLASSES),
                in_=scale_words[:, 4 * quadrant : 4 * quadrant + 4, :].rearrange("c r w -> r c w"),
            )
        pm_codes = const.tile([P, J], U32, align_bytes=64)
        nc.scalar.dma_start(
            out=pm_codes[:].bitcast(F32).rearrange("p (c m) -> p c m", c=N_CLASSES),
            in_=proto_mean_words.rearrange("c p m t -> p c (m t)").bitcast(F32),
        )
        for s in range(1, N_PAIRS):
            if s + 1 < N_PAIRS:
                load_x_var(s + 1)
            load_x(s)

        def row_sums(sums, source):
            for t in range(PAIR):
                folded = work.tile([P, D // 2], F32, name="folded")
                nc.vector.scalar_tensor_tensor(
                    out=folded[:],
                    in0=source[:, t, 0 : D // 2],
                    scalar=1.0,
                    in1=source[:, t, D // 2 : D],
                    op0=ALU.mult,
                    op1=ALU.add,
                    accum_out=sums[:, t : t + 1],
                )

        def transpose_words(bank, source, interleaved):
            words = source[:].bitcast(F32)
            for i in range(PAIR):
                for u in range(HALVES):
                    if interleaved:
                        picked = words[:, i, u:WORDS:HALVES]
                    else:
                        picked = words[:, i, u * P : (u + 1) * P]
                    nc.tensor.transpose(bank[:, u, i * P : (i + 1) * P], picked, identity[:])

        def quantise(pool, grouped, name):
            columns = grouped.shape[1]
            codes = pool.tile([P, columns], U32, name=name + "_codes", align_bytes=64)
            scales = pool.tile([P, columns], U8, name=name + "_scales", align_bytes=64)
            nc.vector.quantize_mx(
                out=codes[:].bitcast(FP8X4),
                scales=scales[:],
                in_=grouped[:].rearrange("p r t -> p (r t)"),
            )
            return codes, scales

        def sqrt_transposed(grouped, source, scale):
            bank = psum.tile([P, HALVES, PAIR_COLS], F32, name="var_bank")
            transpose_words(bank, source, interleaved=False)
            nc.scalar.activation(
                out=grouped.rearrange("p r (u e) -> p r u e", e=2),
                in_=bank[:].bitcast(BF16).rearrange("p u (r e) -> p r u e", e=2),
                func=ACT.Sqrt,
                scale=scale,
            )

        pv_grouped = const.tile([P, PAIR_COLS, 2 * HALVES], BF16, align_bytes=64)
        sqrt_transposed(pv_grouped[:], pv_rows, 4.0 * LAMDA * LAMDA)
        sp = const.tile([P, PAIR], F32)
        row_sums(sp, pv_rows)

        grouped_of = {}
        codes_of = {}
        bias_of = {}

        def transpose_pair(s):
            grouped = work.tile([P, 2 * PAIR_COLS, 2 * HALVES], BF16, name="grouped", align_bytes=64)
            sqrt_transposed(grouped[:, 0:PAIR_COLS, :], xv_rows[s], 1.0)
            x_bank = psum.tile([P, HALVES, PAIR_COLS], F32, name="x_bank")
            transpose_words(x_bank, x_rows[s], interleaved=True)
            nc.scalar.copy(
                out=grouped[:, PAIR_COLS : 2 * PAIR_COLS, :].bitcast(F32),
                in_=x_bank[:].rearrange("p u r -> p r u"),
            )
            grouped_of[s] = grouped

        def bias_pair(s):
            sx = small.tile([P, PAIR], F32, name="sx")
            row_sums(sx, xv_rows[s])
            row_bias = small.tile([P, PAIR], F32, name="row_bias")
            nc.gpsimd.tensor_scalar_mul(out=row_bias[:], in0=sx[:], scalar1=-LAMDA)
            bias_of[s] = row_bias

        def quantise_pair(s):
            codes_of[s] = quantise(work, grouped_of[s], "pixel")

        def multiply_pair(s):
            codes, scales = codes_of[s]
            acc = psum_acc.tile([P, PAIR, J], F32, name="acc")
            for i in range(PAIR):
                xv_cols = slice(i * P, (i + 1) * P)
                x_cols = slice(PAIR_COLS + i * P, PAIR_COLS + (i + 1) * P)
                for first in (True, False):
                    nc.tensor.matmul_mx(
                        out=acc[:, i, :],
                        lhsT=codes[:, x_cols].bitcast(FP8X4),
                        lhsT_scale=scales[:, x_cols],
                        rhs=pm_codes[:].bitcast(FP8X4),
                        rhs_scale=pm_scales[:],
                        start=first,
                        stop=False,
                    )
                nc.tensor.matmul_mx(
                    out=acc[:, i, :],
                    lhsT=codes[:, xv_cols].bitcast(FP8X4),
                    lhsT_scale=scales[:, xv_cols],
                    rhs=pv_codes[:].bitcast(FP8X4),
                    rhs_scale=pv_scales[:],
                    start=False,
                    stop=True,
                )
            result = work.tile([P, PAIR, J], F32, name="result")
            for t in range(PAIR):
                nc.vector.scalar_tensor_tensor(
                    out=result[:, t, :],
                    in0=acc[:, t, :],
                    scalar=bias_of[s][:, t : t + 1],
                    in1=col_bias[:],
                    op0=ALU.add,
                    op1=ALU.add,
                )
            nc.sync.dma_start(out=out_pairs[s], in_=result[:])

        bias_pair(0)
        transpose_pair(0)

        sp_bias = const.tile([P, PAIR], F32)
        nc.vector.tensor_scalar(
            out=sp_bias[:], in0=sp[:], scalar1=-LAMDA, scalar2=-2.0, op0=ALU.mult, op1=ALU.add
        )
        col_bank = psum_once.tile([P, J], F32)
        for i in range(PAIR):
            nc.tensor.transpose(
                col_bank[:, i * P : (i + 1) * P],
                sp_bias[:, i : i + 1].to_broadcast([P, P]),
                identity[:],
            )
        bias_pair(1)
        pv_codes, pv_scales = quantise(const, pv_grouped, "pv")
        col_bias = const.tile([P, J], F32)
        nc.vector.tensor_copy(out=col_bias[:], in_=col_bank[:])

        for s in range(N_PAIRS + 2):
            if s + 1 < N_PAIRS:
                transpose_pair(s + 1)
            if s + 2 < N_PAIRS:
                bias_pair(s + 2)
            if s < N_PAIRS:
                quantise_pair(s)
            if s >= 2:
                multiply_pair(s - 2)
